import numpy as np
import ml_dtypes

BF16 = ml_dtypes.bfloat16


def bf(x):
    return np.asarray(x, np.float32).astype(BF16)


def f32(x):
    return np.asarray(x, np.float32)


def f64(x):
    return np.asarray(x).astype(np.float64)


def striped(idx):
    return np.tile(idx.reshape(-1, 16).T, (8, 1))


S, D, R, M, H, N = 2048, 128, 128, 256, 512, 2048


def sigmoid(v):
    return 1.0 / (1.0 + np.exp(-v))


def elu(v):
    return np.maximum(v, 0.0) + np.exp(np.minimum(v, 0.0)) - 1.0


def setup_inputs():
    return {"table": bf(np.random.standard_normal((D, S))), "w": bf(np.random.standard_normal((D, M)) / np.sqrt(D)), "b_gate": f32(0.1 * np.random.standard_normal((M, 1))), "w_skip": bf(2.0 * np.random.standard_normal((R, H)) / np.sqrt(R)), "b_skip": f32(0.1 * np.random.standard_normal((H, 1))), "w_p1": bf(2.0 * np.random.standard_normal((H, H)) / np.sqrt(H)), "b_p1": f32(0.1 * np.random.standard_normal((H, 1))), "offs": striped(np.random.permutation(np.tile(np.arange(S), 2))[:N])}


def reference(table, w, b_gate, w_skip, b_skip, w_p1, b_p1, offs):
    idx = offs[:16].T.reshape(-1)
    z = f64(w).T @ f64(table)[:, idx] + f64(b_gate)
    u = sigmoid(z[:R]) * np.tanh(z[R:])
    s = f64(w_skip).T @ u + f64(b_skip)
    return elu(f64(w_p1).T @ elu(s) + f64(b_p1))

@@ -1,0 +1,84 @@
+import concourse.mybir as mybir
+
+BF16, F32, U16 = mybir.dt.bfloat16, mybir.dt.float32, mybir.dt.uint16
+ACT = mybir.ActivationFunctionType
+ALU = mybir.AluOpType
+
+P = 128
+LEVELS = 2048
+N = 2048
+PIECE = 512
+N_PIECES = N // PIECE
+HIDDEN = 512
+BLOCKS = HIDDEN // P
+
+FLOPS = 2 * N * (P * 2 * P + P * HIDDEN + HIDDEN * HIDDEN)
+
+
+def tile_wavenetmodel_kernel(tc, table, w, b_gate, w_skip, b_skip, w_p1, b_p1, offs, out):
+    nc = tc.nc
+    with (
+        tc.tile_pool(name="held", bufs=1) as held,
+        tc.tile_pool(name="gated", bufs=N_PIECES) as gated,
+        tc.tile_pool(name="hidden", bufs=2) as hidden,
+        tc.tile_pool(name="work", bufs=4) as work,
+        tc.psum_pool(name="banks", bufs=8) as banks,
+    ):
+        offsets = held.tile([P, N // 16], U16, name="offsets")
+        nc.sync.dma_start(offsets[:], offs)
+        table_sb = held.tile([P, LEVELS], BF16, name="table_sb")
+        nc.sync.dma_start(table_sb[:], table)
+        w_sb = held.tile([P, 2 * P], BF16, name="w_sb")
+        nc.scalar.dma_start(w_sb[:], w)
+        w_skip_sb = held.tile([P, HIDDEN], BF16, name="w_skip_sb")
+        nc.scalar.dma_start(w_skip_sb[:], w_skip)
+        w_p1_sb = held.tile([P, BLOCKS, HIDDEN], BF16, name="w_p1_sb")
+        nc.gpsimd.dma_start(w_p1_sb[:], w_p1.rearrange("(k p) q -> p k q", p=P))
+        b_gate_sb = held.tile([P, 2], F32, name="b_gate_sb")
+        b_skip_sb = held.tile([P, BLOCKS], F32, name="b_skip_sb")
+        b_p1_sb = held.tile([P, BLOCKS], F32, name="b_p1_sb")
+        with nc.allow_non_contiguous_dma(reason="a bias vector goes one element to a partition"):
+            nc.scalar.dma_start(b_gate_sb[:], b_gate.rearrange("(k p) one -> p (k one)", p=P))
+            nc.gpsimd.dma_start(b_skip_sb[:], b_skip.rearrange("(k p) one -> p (k one)", p=P))
+            nc.gpsimd.dma_start(b_p1_sb[:], b_p1.rearrange("(k p) one -> p (k one)", p=P))
+
+        def elu(result, acc, bias):
+            grown = work.tile([P, PIECE], F32, name="grown")
+            nc.scalar.activation(grown[:], acc, ACT.Exp, bias=bias)
+            below = work.tile([P, PIECE], F32, name="below")
+            nc.vector.tensor_scalar(below[:], grown[:], 1.0, -1.0, op0=ALU.min, op1=ALU.add)
+            nc.vector.scalar_tensor_tensor(result, acc, bias, below[:], op0=ALU.add, op1=ALU.max)
+
+        u = []
+        for c in range(N_PIECES):
+            piece_offsets = offsets[:, c * (PIECE // 16) : (c + 1) * (PIECE // 16)]
+            z_sigmoid = banks.tile([P, PIECE], F32, name="z_sigmoid", tag="bank")
+            nc.tensor.matmul(z_sigmoid[:], w_sb[:, 0:P], table_sb[:].indirect(piece_offsets), start=True, stop=True)
+            z_tanh = banks.tile([P, PIECE], F32, name="z_tanh", tag="bank")
+            nc.tensor.matmul(z_tanh[:], w_sb[:, P : 2 * P], table_sb[:].indirect(piece_offsets), start=True, stop=True)
+            gate = work.tile([P, PIECE], F32, name="gate")
+            nc.scalar.activation(gate[:], z_sigmoid[:], ACT.Sigmoid, bias=b_gate_sb[:, 0:1])
+            signal = work.tile([P, PIECE], F32, name="signal")
+            nc.scalar.activation(signal[:], z_tanh[:], ACT.Tanh, bias=b_gate_sb[:, 1:2])
+            u_piece = gated.tile([P, PIECE], BF16, name="u_piece")
+            nc.vector.tensor_tensor(u_piece[:], gate[:], signal[:], ALU.mult)
+            u.append(u_piece)
+
+        for c in range(N_PIECES):
+            h = []
+            for k in range(BLOCKS):
+                s = banks.tile([P, PIECE], F32, name="s", tag="bank")
+                nc.tensor.matmul(s[:], w_skip_sb[:, k * P : (k + 1) * P], u[c][:], start=True, stop=True)
+                h_block = hidden.tile([P, PIECE], BF16, name=f"h{k}")
+                elu(h_block[:], s[:], b_skip_sb[:, k : k + 1])
+                h.append(h_block)
+            acc = [banks.tile([P, PIECE], F32, name=f"acc{q}", tag="bank") for q in range(BLOCKS)]
+            for k in range(BLOCKS):
+                for q in range(BLOCKS):
+                    nc.tensor.matmul(
+                        acc[q][:], w_p1_sb[:, k, q * P : (q + 1) * P], h[k][:], start=(k == 0), stop=(k == BLOCKS - 1)
+                    )
+            for q in range(BLOCKS):
+                o = work.tile([P, PIECE], F32, name="o")
+                elu(o[:], acc[q][:], b_p1_sb[:, q : q + 1])
+                nc.sync.dma_start(out[q * P : (q + 1) * P, c * PIECE : (c + 1) * PIECE], o[:])

@@ -33,14 +33,19 @@ def tile_wavenetmodel_kernel(tc, table, w, b_gate, w_skip, b_skip, w_p1, b_p1, o
         w_skip_sb = held.tile([P, HIDDEN], BF16, name="w_skip_sb")
         nc.scalar.dma_start(w_skip_sb[:], w_skip)
         w_p1_sb = held.tile([P, BLOCKS, HIDDEN], BF16, name="w_p1_sb")
-        nc.gpsimd.dma_start(w_p1_sb[:], w_p1.rearrange("(k p) q -> p k q", p=P))
+        nc.sync.dma_start(w_p1_sb[:], w_p1.rearrange("(k p) q -> p k q", p=P))
         b_gate_sb = held.tile([P, 2], F32, name="b_gate_sb")
         b_skip_sb = held.tile([P, BLOCKS], F32, name="b_skip_sb")
         b_p1_sb = held.tile([P, BLOCKS], F32, name="b_p1_sb")
         with nc.allow_non_contiguous_dma(reason="a bias vector goes one element to a partition"):
             nc.scalar.dma_start(b_gate_sb[:], b_gate.rearrange("(k p) one -> p (k one)", p=P))
-            nc.gpsimd.dma_start(b_skip_sb[:], b_skip.rearrange("(k p) one -> p (k one)", p=P))
-            nc.gpsimd.dma_start(b_p1_sb[:], b_p1.rearrange("(k p) one -> p (k one)", p=P))
+            nc.scalar.dma_start(b_skip_sb[:], b_skip.rearrange("(k p) one -> p (k one)", p=P))
+            nc.scalar.dma_start(b_p1_sb[:], b_p1.rearrange("(k p) one -> p (k one)", p=P))
+
+        w_skip_half = held.tile([P, HIDDEN], BF16, name="w_skip_half")
+        nc.vector.tensor_scalar_mul(w_skip_half[:], w_skip_sb[:], 0.5)
+        b_sigmoid_half = held.tile([P, 1], F32, name="b_sigmoid_half")
+        nc.vector.tensor_scalar_mul(b_sigmoid_half[:], b_gate_sb[:, 0:1], 0.5)
 
         def elu(result, acc, bias):
             grown = work.tile([P, PIECE], F32, name="grown")
@@ -49,36 +54,47 @@ def tile_wavenetmodel_kernel(tc, table, w, b_gate, w_skip, b_skip, w_p1, b_p1, o
             nc.vector.tensor_scalar(below[:], grown[:], 1.0, -1.0, op0=ALU.min, op1=ALU.add)
             nc.vector.scalar_tensor_tensor(result, acc, bias, below[:], op0=ALU.add, op1=ALU.max)
 
-        u = []
-        for c in range(N_PIECES):
+        def gate(c):
             piece_offsets = offsets[:, c * (PIECE // 16) : (c + 1) * (PIECE // 16)]
             z_sigmoid = banks.tile([P, PIECE], F32, name="z_sigmoid", tag="bank")
             nc.tensor.matmul(z_sigmoid[:], w_sb[:, 0:P], table_sb[:].indirect(piece_offsets), start=True, stop=True)
             z_tanh = banks.tile([P, PIECE], F32, name="z_tanh", tag="bank")
             nc.tensor.matmul(z_tanh[:], w_sb[:, P : 2 * P], table_sb[:].indirect(piece_offsets), start=True, stop=True)
-            gate = work.tile([P, PIECE], F32, name="gate")
-            nc.scalar.activation(gate[:], z_sigmoid[:], ACT.Sigmoid, bias=b_gate_sb[:, 0:1])
+            opening = work.tile([P, PIECE], F32, name="opening")
+            nc.scalar.activation(opening[:], z_sigmoid[:], ACT.Tanh, bias=b_sigmoid_half[:], scale=0.5)
             signal = work.tile([P, PIECE], F32, name="signal")
             nc.scalar.activation(signal[:], z_tanh[:], ACT.Tanh, bias=b_gate_sb[:, 1:2])
-            u_piece = gated.tile([P, PIECE], BF16, name="u_piece")
-            nc.vector.tensor_tensor(u_piece[:], gate[:], signal[:], ALU.mult)
-            u.append(u_piece)
+            u_twice = gated.tile([P, PIECE], BF16, name="u_twice")
+            nc.vector.scalar_tensor_tensor(u_twice[:], opening[:], 1.0, signal[:], op0=ALU.add, op1=ALU.mult)
+            return u_twice
 
-        for c in range(N_PIECES):
+        def skip(u_twice):
             h = []
             for k in range(BLOCKS):
                 s = banks.tile([P, PIECE], F32, name="s", tag="bank")
-                nc.tensor.matmul(s[:], w_skip_sb[:, k * P : (k + 1) * P], u[c][:], start=True, stop=True)
+                nc.tensor.matmul(s[:], w_skip_half[:, k * P : (k + 1) * P], u_twice[:], start=True, stop=True)
                 h_block = hidden.tile([P, PIECE], BF16, name=f"h{k}")
                 elu(h_block[:], s[:], b_skip_sb[:, k : k + 1])
                 h.append(h_block)
-            acc = [banks.tile([P, PIECE], F32, name=f"acc{q}", tag="bank") for q in range(BLOCKS)]
-            for k in range(BLOCKS):
-                for q in range(BLOCKS):
-                    nc.tensor.matmul(
-                        acc[q][:], w_p1_sb[:, k, q * P : (q + 1) * P], h[k][:], start=(k == 0), stop=(k == BLOCKS - 1)
-                    )
+            return h
+
+        def post(c, h):
             for q in range(BLOCKS):
+                acc = banks.tile([P, PIECE], F32, name="acc", tag="bank")
+                for k in range(BLOCKS):
+                    nc.tensor.matmul(
+                        acc[:], w_p1_sb[:, k, q * P : (q + 1) * P], h[k][:], start=(k == 0), stop=(k == BLOCKS - 1)
+                    )
                 o = work.tile([P, PIECE], F32, name="o")
-                elu(o[:], acc[q][:], b_p1_sb[:, q : q + 1])
+                elu(o[:], acc[:], b_p1_sb[:, q : q + 1])
                 nc.sync.dma_start(out[q * P : (q + 1) * P, c * PIECE : (c + 1) * PIECE], o[:])
+
+        u_twice = {0: gate(0), 1: gate(1)}
+        h = {0: skip(u_twice[0]), 1: skip(u_twice[1])}
+        post(0, h[0])
+        u_twice[2], u_twice[3] = gate(2), gate(3)
+        h[2] = skip(u_twice[2])
+        post(1, h[1])
+        h[3] = skip(u_twice[3])
+        post(2, h[2])
+        post(3, h[3])

@@ -25,34 +25,38 @@ def tile_wavenetmodel_kernel(tc, table, w, b_gate, w_skip, b_skip, w_p1, b_p1, o
         tc.psum_pool(name="banks", bufs=8) as banks,
     ):
         offsets = held.tile([P, N // 16], U16, name="offsets")
-        nc.sync.dma_start(offsets[:], offs)
         table_sb = held.tile([P, LEVELS], BF16, name="table_sb")
-        nc.sync.dma_start(table_sb[:], table)
         w_sb = held.tile([P, 2 * P], BF16, name="w_sb")
-        nc.scalar.dma_start(w_sb[:], w)
-        w_skip_sb = held.tile([P, HIDDEN], BF16, name="w_skip_sb")
-        nc.scalar.dma_start(w_skip_sb[:], w_skip)
-        w_p1_sb = held.tile([P, BLOCKS, HIDDEN], BF16, name="w_p1_sb")
-        nc.sync.dma_start(w_p1_sb[:], w_p1.rearrange("(k p) q -> p k q", p=P))
         b_gate_sb = held.tile([P, 2], F32, name="b_gate_sb")
+        w_skip_sb = held.tile([P, HIDDEN], BF16, name="w_skip_sb")
         b_skip_sb = held.tile([P, BLOCKS], F32, name="b_skip_sb")
+        w_p1_sb = held.tile([P, BLOCKS, HIDDEN], BF16, name="w_p1_sb")
         b_p1_sb = held.tile([P, BLOCKS], F32, name="b_p1_sb")
+        nc.sync.dma_start(offsets[:], offs)
+        nc.sync.dma_start(table_sb[:], table)
         with nc.allow_non_contiguous_dma(reason="a bias vector goes one element to a partition"):
             nc.scalar.dma_start(b_gate_sb[:], b_gate.rearrange("(k p) one -> p (k one)", p=P))
-            nc.scalar.dma_start(b_skip_sb[:], b_skip.rearrange("(k p) one -> p (k one)", p=P))
-            nc.scalar.dma_start(b_p1_sb[:], b_p1.rearrange("(k p) one -> p (k one)", p=P))
+            nc.gpsimd.dma_start(b_skip_sb[:], b_skip.rearrange("(k p) one -> p (k one)", p=P))
+            nc.gpsimd.dma_start(b_p1_sb[:], b_p1.rearrange("(k p) one -> p (k one)", p=P))
+        nc.scalar.dma_start(w_sb[:], w)
+        nc.sync.dma_start(w_skip_sb[:], w_skip)
+        nc.sync.dma_start(w_p1_sb[:], w_p1.rearrange("(k p) q -> p k q", p=P))
 
         w_skip_half = held.tile([P, HIDDEN], BF16, name="w_skip_half")
         nc.vector.tensor_scalar_mul(w_skip_half[:], w_skip_sb[:], 0.5)
         b_sigmoid_half = held.tile([P, 1], F32, name="b_sigmoid_half")
         nc.vector.tensor_scalar_mul(b_sigmoid_half[:], b_gate_sb[:, 0:1], 0.5)
 
-        def elu(result, acc, bias):
+        def elu(result, acc, bias, spare_vector):
             grown = work.tile([P, PIECE], F32, name="grown")
             nc.scalar.activation(grown[:], acc, ACT.Exp, bias=bias)
-            below = work.tile([P, PIECE], F32, name="below")
-            nc.vector.tensor_scalar(below[:], grown[:], 1.0, -1.0, op0=ALU.min, op1=ALU.add)
-            nc.vector.scalar_tensor_tensor(result, acc, bias, below[:], op0=ALU.add, op1=ALU.max)
+            other = work.tile([P, PIECE], F32, name="other")
+            if spare_vector:
+                nc.scalar.activation(other[:], acc, ACT.Relu, bias=bias)
+                nc.vector.scalar_tensor_tensor(result, grown[:], -1.0, other[:], op0=ALU.add, op1=ALU.min)
+            else:
+                nc.vector.tensor_scalar(other[:], grown[:], 1.0, -1.0, op0=ALU.min, op1=ALU.add)
+                nc.vector.scalar_tensor_tensor(result, acc, bias, other[:], op0=ALU.add, op1=ALU.max)
 
         def gate(c):
             piece_offsets = offsets[:, c * (PIECE // 16) : (c + 1) * (PIECE // 16)]
@@ -74,7 +78,7 @@ def tile_wavenetmodel_kernel(tc, table, w, b_gate, w_skip, b_skip, w_p1, b_p1, o
                 s = banks.tile([P, PIECE], F32, name="s", tag="bank")
                 nc.tensor.matmul(s[:], w_skip_half[:, k * P : (k + 1) * P], u_twice[:], start=True, stop=True)
                 h_block = hidden.tile([P, PIECE], BF16, name=f"h{k}")
-                elu(h_block[:], s[:], b_skip_sb[:, k : k + 1])
+                elu(h_block[:], s[:], b_skip_sb[:, k : k + 1], spare_vector=(k == BLOCKS - 1))
                 h.append(h_block)
             return h
 
@@ -86,15 +90,12 @@ def tile_wavenetmodel_kernel(tc, table, w, b_gate, w_skip, b_skip, w_p1, b_p1, o
                         acc[:], w_p1_sb[:, k, q * P : (q + 1) * P], h[k][:], start=(k == 0), stop=(k == BLOCKS - 1)
                     )
                 o = work.tile([P, PIECE], F32, name="o")
-                elu(o[:], acc[:], b_p1_sb[:, q : q + 1])
+                elu(o[:], acc[:], b_p1_sb[:, q : q + 1], spare_vector=(q == BLOCKS - 1))
                 nc.sync.dma_start(out[q * P : (q + 1) * P, c * PIECE : (c + 1) * PIECE], o[:])
 
-        u_twice = {0: gate(0), 1: gate(1)}
-        h = {0: skip(u_twice[0]), 1: skip(u_twice[1])}
-        post(0, h[0])
-        u_twice[2], u_twice[3] = gate(2), gate(3)
-        h[2] = skip(u_twice[2])
-        post(1, h[1])
-        h[3] = skip(u_twice[3])
-        post(2, h[2])
-        post(3, h[3])
+        u_twice = [gate(c) for c in range(N_PIECES)]
+        h = {0: skip(u_twice[0])}
+        for c in range(N_PIECES):
+            if c + 1 < N_PIECES:
+                h[c + 1] = skip(u_twice[c + 1])
+            post(c, h[c])

@@ -11,6 +11,7 @@ PIECE = 512
 N_PIECES = N // PIECE
 HIDDEN = 512
 BLOCKS = HIDDEN // P
+WARM_UP = 6
 
 FLOPS = 2 * N * (P * 2 * P + P * HIDDEN + HIDDEN * HIDDEN)
 
@@ -41,6 +42,12 @@ def tile_wavenetmodel_kernel(tc, table, w, b_gate, w_skip, b_skip, w_p1, b_p1, o
         nc.scalar.dma_start(w_sb[:], w)
         nc.sync.dma_start(w_skip_sb[:], w_skip)
         nc.sync.dma_start(w_p1_sb[:], w_p1.rearrange("(k p) q -> p k q", p=P))
+
+        zeros = held.tile([P, PIECE], BF16, name="zeros")
+        nc.vector.memset(zeros[:], 0.0)
+        unused = banks.tile([P, PIECE], F32, name="unused", tag="bank")
+        for i in range(WARM_UP):
+            nc.tensor.matmul(unused[:], zeros[:, 0:P], zeros[:], start=True, stop=True)
 
         w_skip_half = held.tile([P, HIDDEN], BF16, name="w_skip_half")
         nc.vector.tensor_scalar_mul(w_skip_half[:], w_skip_sb[:], 0.5)

@@ -11,7 +11,6 @@ PIECE = 512
 N_PIECES = N // PIECE
 HIDDEN = 512
 BLOCKS = HIDDEN // P
-WARM_UP = 6
 
 FLOPS = 2 * N * (P * 2 * P + P * HIDDEN + HIDDEN * HIDDEN)
 
@@ -43,27 +42,33 @@ def tile_wavenetmodel_kernel(tc, table, w, b_gate, w_skip, b_skip, w_p1, b_p1, o
         nc.sync.dma_start(w_skip_sb[:], w_skip)
         nc.sync.dma_start(w_p1_sb[:], w_p1.rearrange("(k p) q -> p k q", p=P))
 
-        zeros = held.tile([P, PIECE], BF16, name="zeros")
-        nc.vector.memset(zeros[:], 0.0)
-        unused = banks.tile([P, PIECE], F32, name="unused", tag="bank")
-        for i in range(WARM_UP):
-            nc.tensor.matmul(unused[:], zeros[:, 0:P], zeros[:], start=True, stop=True)
-
         w_skip_half = held.tile([P, HIDDEN], BF16, name="w_skip_half")
         nc.vector.tensor_scalar_mul(w_skip_half[:], w_skip_sb[:], 0.5)
         b_sigmoid_half = held.tile([P, 1], F32, name="b_sigmoid_half")
         nc.vector.tensor_scalar_mul(b_sigmoid_half[:], b_gate_sb[:, 0:1], 0.5)
 
-        def elu(result, acc, bias, spare_vector):
+        def elu_first(acc, bias, spare_vector):
             grown = work.tile([P, PIECE], F32, name="grown")
             nc.scalar.activation(grown[:], acc, ACT.Exp, bias=bias)
             other = work.tile([P, PIECE], F32, name="other")
             if spare_vector:
                 nc.scalar.activation(other[:], acc, ACT.Relu, bias=bias)
-                nc.vector.scalar_tensor_tensor(result, grown[:], -1.0, other[:], op0=ALU.add, op1=ALU.min)
             else:
                 nc.vector.tensor_scalar(other[:], grown[:], 1.0, -1.0, op0=ALU.min, op1=ALU.add)
+            return grown, other
+
+        def elu_last(result, acc, bias, grown, other, spare_vector):
+            if spare_vector:
+                nc.vector.scalar_tensor_tensor(result, grown[:], -1.0, other[:], op0=ALU.add, op1=ALU.min)
+            else:
                 nc.vector.scalar_tensor_tensor(result, acc, bias, other[:], op0=ALU.add, op1=ALU.max)
+
+        def staggered(first, last):
+            for k in range(BLOCKS + 1):
+                if k < BLOCKS:
+                    first(k)
+                if k > 0:
+                    last(k - 1)
 
         def gate(c):
             piece_offsets = offsets[:, c * (PIECE // 16) : (c + 1) * (PIECE // 16)]
@@ -80,25 +85,37 @@ def tile_wavenetmodel_kernel(tc, table, w, b_gate, w_skip, b_skip, w_p1, b_p1, o
             return u_twice
 
         def skip(u_twice):
-            h = []
-            for k in range(BLOCKS):
-                s = banks.tile([P, PIECE], F32, name="s", tag="bank")
-                nc.tensor.matmul(s[:], w_skip_half[:, k * P : (k + 1) * P], u_twice[:], start=True, stop=True)
-                h_block = hidden.tile([P, PIECE], BF16, name=f"h{k}")
-                elu(h_block[:], s[:], b_skip_sb[:, k : k + 1], spare_vector=(k == BLOCKS - 1))
-                h.append(h_block)
+            s, terms, h = {}, {}, {}
+
+            def first(k):
+                s[k] = banks.tile([P, PIECE], F32, name="s", tag="bank")
+                nc.tensor.matmul(s[k][:], w_skip_half[:, k * P : (k + 1) * P], u_twice[:], start=True, stop=True)
+                terms[k] = elu_first(s[k][:], b_skip_sb[:, k : k + 1], k == BLOCKS - 1)
+
+            def last(k):
+                h[k] = hidden.tile([P, PIECE], BF16, name=f"h{k}")
+                elu_last(h[k][:], s[k][:], b_skip_sb[:, k : k + 1], terms[k][0], terms[k][1], k == BLOCKS - 1)
+
+            staggered(first, last)
             return h
 
         def post(c, h):
-            for q in range(BLOCKS):
-                acc = banks.tile([P, PIECE], F32, name="acc", tag="bank")
+            acc, terms = {}, {}
+
+            def first(q):
+                acc[q] = banks.tile([P, PIECE], F32, name="acc", tag="bank")
                 for k in range(BLOCKS):
                     nc.tensor.matmul(
-                        acc[:], w_p1_sb[:, k, q * P : (q + 1) * P], h[k][:], start=(k == 0), stop=(k == BLOCKS - 1)
+                        acc[q][:], w_p1_sb[:, k, q * P : (q + 1) * P], h[k][:], start=(k == 0), stop=(k == BLOCKS - 1)
                     )
+                terms[q] = elu_first(acc[q][:], b_p1_sb[:, q : q + 1], q == BLOCKS - 1)
+
+            def last(q):
                 o = work.tile([P, PIECE], F32, name="o")
-                elu(o[:], acc[:], b_p1_sb[:, q : q + 1], spare_vector=(q == BLOCKS - 1))
+                elu_last(o[:], acc[q][:], b_p1_sb[:, q : q + 1], terms[q][0], terms[q][1], q == BLOCKS - 1)
                 nc.sync.dma_start(out[q * P : (q + 1) * P, c * PIECE : (c + 1) * PIECE], o[:])
+
+            staggered(first, last)
 
         u_twice = [gate(c) for c in range(N_PIECES)]
         h = {0: skip(u_twice[0])}

@@ -47,10 +47,10 @@ def tile_wavenetmodel_kernel(tc, table, w, b_gate, w_skip, b_skip, w_p1, b_p1, o
         b_sigmoid_half = held.tile([P, 1], F32, name="b_sigmoid_half")
         nc.vector.tensor_scalar_mul(b_sigmoid_half[:], b_gate_sb[:, 0:1], 0.5)
 
-        def elu_first(acc, bias, spare_vector):
-            grown = work.tile([P, PIECE], F32, name="grown")
+        def elu_first(acc, bias, spare_vector, width=PIECE):
+            grown = work.tile([P, width], F32, name="grown")
             nc.scalar.activation(grown[:], acc, ACT.Exp, bias=bias)
-            other = work.tile([P, PIECE], F32, name="other")
+            other = work.tile([P, width], F32, name="other")
             if spare_vector:
                 nc.scalar.activation(other[:], acc, ACT.Relu, bias=bias)
             else:
@@ -101,6 +101,9 @@ def tile_wavenetmodel_kernel(tc, table, w, b_gate, w_skip, b_skip, w_p1, b_p1, o
 
         def post(c, h):
             acc, terms = {}, {}
+            last_piece = c == N_PIECES - 1
+            spares = [q == BLOCKS - 1 or (last_piece and q % 2 == 1) for q in range(BLOCKS)]
+            widths = [PIECE // 2 if last_piece and q == BLOCKS - 1 else PIECE for q in range(BLOCKS)]
 
             def first(q):
                 acc[q] = banks.tile([P, PIECE], F32, name="acc", tag="bank")
@@ -108,18 +111,26 @@ def tile_wavenetmodel_kernel(tc, table, w, b_gate, w_skip, b_skip, w_p1, b_p1, o
                     nc.tensor.matmul(
                         acc[q][:], w_p1_sb[:, k, q * P : (q + 1) * P], h[k][:], start=(k == 0), stop=(k == BLOCKS - 1)
                     )
-                terms[q] = elu_first(acc[q][:], b_p1_sb[:, q : q + 1], q == BLOCKS - 1)
+                terms[q] = [
+                    elu_first(acc[q][:, j : j + widths[q]], b_p1_sb[:, q : q + 1], spares[q], widths[q])
+                    for j in range(0, PIECE, widths[q])
+                ]
 
             def last(q):
-                o = work.tile([P, PIECE], F32, name="o")
-                elu_last(o[:], acc[q][:], b_p1_sb[:, q : q + 1], terms[q][0], terms[q][1], q == BLOCKS - 1)
-                nc.sync.dma_start(out[q * P : (q + 1) * P, c * PIECE : (c + 1) * PIECE], o[:])
+                for i, (grown, other) in enumerate(terms[q]):
+                    j = i * widths[q]
+                    o = work.tile([P, widths[q]], F32, name="o")
+                    elu_last(o[:], acc[q][:, j : j + widths[q]], b_p1_sb[:, q : q + 1], grown, other, spares[q])
+                    column = c * PIECE + j
+                    nc.sync.dma_start(out[q * P : (q + 1) * P, column : column + widths[q]], o[:])
 
             staggered(first, last)
 
-        u_twice = [gate(c) for c in range(N_PIECES)]
+        u_twice = {c: gate(c) for c in range(N_PIECES - 1)}
         h = {0: skip(u_twice[0])}
         for c in range(N_PIECES):
             if c + 1 < N_PIECES:
                 h[c + 1] = skip(u_twice[c + 1])
+            if c == 1:
+                u_twice[N_PIECES - 1] = gate(N_PIECES - 1)
             post(c, h[c])

@@ -22,6 +22,7 @@ def tile_wavenetmodel_kernel(tc, table, w, b_gate, w_skip, b_skip, w_p1, b_p1, o
         tc.tile_pool(name="gated", bufs=N_PIECES) as gated,
         tc.tile_pool(name="hidden", bufs=2) as hidden,
         tc.tile_pool(name="work", bufs=4) as work,
+        tc.tile_pool(name="outputs", bufs=8) as outputs,
         tc.psum_pool(name="banks", bufs=8) as banks,
     ):
         offsets = held.tile([P, N // 16], U16, name="offsets")
@@ -119,7 +120,7 @@ def tile_wavenetmodel_kernel(tc, table, w, b_gate, w_skip, b_skip, w_p1, b_p1, o
             def last(q):
                 for i, (grown, other) in enumerate(terms[q]):
                     j = i * widths[q]
-                    o = work.tile([P, widths[q]], F32, name="o")
+                    o = outputs.tile([P, widths[q]], F32, name="o")
                     elu_last(o[:], acc[q][:, j : j + widths[q]], b_p1_sb[:, q : q + 1], grown, other, spares[q])
                     column = c * PIECE + j
                     nc.sync.dma_start(out[q * P : (q + 1) * P, column : column + widths[q]], o[:])

@@ -35,13 +35,18 @@ def tile_wavenetmodel_kernel(tc, table, w, b_gate, w_skip, b_skip, w_p1, b_p1, o
         b_p1_sb = held.tile([P, BLOCKS], F32, name="b_p1_sb")
         nc.sync.dma_start(offsets[:], offs)
         nc.sync.dma_start(table_sb[:], table)
+        nc.scalar.dma_start(w_sb[:], w)
         with nc.allow_non_contiguous_dma(reason="a bias vector goes one element to a partition"):
             nc.scalar.dma_start(b_gate_sb[:], b_gate.rearrange("(k p) one -> p (k one)", p=P))
             nc.gpsimd.dma_start(b_skip_sb[:], b_skip.rearrange("(k p) one -> p (k one)", p=P))
             nc.gpsimd.dma_start(b_p1_sb[:], b_p1.rearrange("(k p) one -> p (k one)", p=P))
-        nc.scalar.dma_start(w_sb[:], w)
         nc.sync.dma_start(w_skip_sb[:], w_skip)
         nc.sync.dma_start(w_p1_sb[:], w_p1.rearrange("(k p) q -> p k q", p=P))
+
+        zeros = held.tile([P, 1], F32, name="zeros")
+        nc.vector.memset(zeros[:], 0.0)
+        unread = held.tile([P, 1], F32, name="unread")
+        nc.scalar.activation(unread[:], zeros[:], ACT.Tanh)
 
         w_skip_half = held.tile([P, HIDDEN], BF16, name="w_skip_half")
         nc.vector.tensor_scalar_mul(w_skip_half[:], w_skip_sb[:], 0.5)

@@ -9,6 +9,7 @@ LEVELS = 2048
 N = 2048
 PIECE = 512
 N_PIECES = N // PIECE
+STRIP = PIECE // 4
 HIDDEN = 512
 BLOCKS = HIDDEN // P
 
@@ -95,7 +96,14 @@ def tile_wavenetmodel_kernel(tc, table, w, b_gate, w_skip, b_skip, w_p1, b_p1, o
 
             def first(k):
                 s[k] = banks.tile([P, PIECE], F32, name="s", tag="bank")
-                nc.tensor.matmul(s[k][:], w_skip_half[:, k * P : (k + 1) * P], u_twice[:], start=True, stop=True)
+                for j in range(0, PIECE, STRIP):
+                    nc.tensor.matmul(
+                        s[k][:, j : j + STRIP],
+                        w_skip_half[:, k * P : (k + 1) * P],
+                        u_twice[:, j : j + STRIP],
+                        start=True,
+                        stop=True,
+                    )
                 terms[k] = elu_first(s[k][:], b_skip_sb[:, k : k + 1], k == BLOCKS - 1)
 
             def last(k):
@@ -132,11 +140,16 @@ def tile_wavenetmodel_kernel(tc, table, w, b_gate, w_skip, b_skip, w_p1, b_p1, o
 
             staggered(first, last)
 
-        u_twice = {c: gate(c) for c in range(N_PIECES - 1)}
-        h = {0: skip(u_twice[0])}
-        for c in range(N_PIECES):
-            if c + 1 < N_PIECES:
-                h[c + 1] = skip(u_twice[c + 1])
-            if c == 1:
-                u_twice[N_PIECES - 1] = gate(N_PIECES - 1)
-            post(c, h[c])
+        u_twice, h = {}, {}
+        for c in (0, 1):
+            u_twice[c] = gate(c)
+        for c in (0, 1):
+            h[c] = skip(u_twice[c])
+        u_twice[2] = gate(2)
+        post(0, h[0])
+        h[2] = skip(u_twice[2])
+        u_twice[3] = gate(3)
+        post(1, h[1])
+        h[3] = skip(u_twice[3])
+        post(2, h[2])
+        post(3, h[3])

@@ -9,7 +9,6 @@ LEVELS = 2048
 N = 2048
 PIECE = 512
 N_PIECES = N // PIECE
-STRIP = PIECE // 4
 HIDDEN = 512
 BLOCKS = HIDDEN // P
 
@@ -91,16 +90,17 @@ def tile_wavenetmodel_kernel(tc, table, w, b_gate, w_skip, b_skip, w_p1, b_p1, o
             nc.vector.scalar_tensor_tensor(u_twice[:], opening[:], 1.0, signal[:], op0=ALU.add, op1=ALU.mult)
             return u_twice
 
-        def skip(u_twice):
+        def skip(u_twice, strips):
+            width = PIECE // strips
             s, terms, h = {}, {}, {}
 
             def first(k):
                 s[k] = banks.tile([P, PIECE], F32, name="s", tag="bank")
-                for j in range(0, PIECE, STRIP):
+                for j in range(0, PIECE, width):
                     nc.tensor.matmul(
-                        s[k][:, j : j + STRIP],
+                        s[k][:, j : j + width],
                         w_skip_half[:, k * P : (k + 1) * P],
-                        u_twice[:, j : j + STRIP],
+                        u_twice[:, j : j + width],
                         start=True,
                         stop=True,
                     )
@@ -144,12 +144,12 @@ def tile_wavenetmodel_kernel(tc, table, w, b_gate, w_skip, b_skip, w_p1, b_p1, o
         for c in (0, 1):
             u_twice[c] = gate(c)
         for c in (0, 1):
-            h[c] = skip(u_twice[c])
+            h[c] = skip(u_twice[c], strips=4)
         u_twice[2] = gate(2)
         post(0, h[0])
-        h[2] = skip(u_twice[2])
+        h[2] = skip(u_twice[2], strips=2)
         u_twice[3] = gate(3)
         post(1, h[1])
-        h[3] = skip(u_twice[3])
+        h[3] = skip(u_twice[3], strips=1)
         post(2, h[2])
         post(3, h[3])

@@ -20,9 +20,9 @@ def tile_wavenetmodel_kernel(tc, table, w, b_gate, w_skip, b_skip, w_p1, b_p1, o
     with (
         tc.tile_pool(name="held", bufs=1) as held,
         tc.tile_pool(name="gated", bufs=N_PIECES) as gated,
-        tc.tile_pool(name="hidden", bufs=2) as hidden,
-        tc.tile_pool(name="work", bufs=4) as work,
-        tc.tile_pool(name="outputs", bufs=8) as outputs,
+        tc.tile_pool(name="hidden", bufs=N_PIECES) as hidden,
+        tc.tile_pool(name="work", bufs=12) as work,
+        tc.tile_pool(name="outputs", bufs=16) as outputs,
         tc.psum_pool(name="banks", bufs=8) as banks,
     ):
         offsets = held.tile([P, N // 16], U16, name="offsets")
@@ -114,28 +114,30 @@ def tile_wavenetmodel_kernel(tc, table, w, b_gate, w_skip, b_skip, w_p1, b_p1, o
             return h
 
         def post(c, h):
-            acc, terms = {}, {}
+            parts = {}
             last_piece = c == N_PIECES - 1
-            spares = [q == BLOCKS - 1 or (last_piece and q % 2 == 1) for q in range(BLOCKS)]
+            spares = [q == BLOCKS - 1 or (last_piece and q > 0) for q in range(BLOCKS)]
             widths = [PIECE // 2 if last_piece and q == BLOCKS - 1 else PIECE for q in range(BLOCKS)]
 
             def first(q):
-                acc[q] = banks.tile([P, PIECE], F32, name="acc", tag="bank")
-                for k in range(BLOCKS):
-                    nc.tensor.matmul(
-                        acc[q][:], w_p1_sb[:, k, q * P : (q + 1) * P], h[k][:], start=(k == 0), stop=(k == BLOCKS - 1)
-                    )
-                terms[q] = [
-                    elu_first(acc[q][:, j : j + widths[q]], b_p1_sb[:, q : q + 1], spares[q], widths[q])
-                    for j in range(0, PIECE, widths[q])
-                ]
+                parts[q] = []
+                for j in range(0, PIECE, widths[q]):
+                    acc = banks.tile([P, widths[q]], F32, name="acc", tag="bank")
+                    for k in range(BLOCKS):
+                        nc.tensor.matmul(
+                            acc[:],
+                            w_p1_sb[:, k, q * P : (q + 1) * P],
+                            h[k][:, j : j + widths[q]],
+                            start=(k == 0),
+                            stop=(k == BLOCKS - 1),
+                        )
+                    grown, other = elu_first(acc[:], b_p1_sb[:, q : q + 1], spares[q], widths[q])
+                    parts[q].append((c * PIECE + j, acc, grown, other))
 
             def last(q):
-                for i, (grown, other) in enumerate(terms[q]):
-                    j = i * widths[q]
+                for column, acc, grown, other in parts[q]:
                     o = outputs.tile([P, widths[q]], F32, name="o")
-                    elu_last(o[:], acc[q][:, j : j + widths[q]], b_p1_sb[:, q : q + 1], grown, other, spares[q])
-                    column = c * PIECE + j
+                    elu_last(o[:], acc[:], b_p1_sb[:, q : q + 1], grown, other, spares[q])
                     nc.sync.dma_start(out[q * P : (q + 1) * P, column : column + widths[q]], o[:])
 
             staggered(first, last)

@@ -116,7 +116,7 @@ def tile_wavenetmodel_kernel(tc, table, w, b_gate, w_skip, b_skip, w_p1, b_p1, o
         def post(c, h):
             parts = {}
             last_piece = c == N_PIECES - 1
-            spares = [q == BLOCKS - 1 or (last_piece and q > 0) for q in range(BLOCKS)]
+            spares = [q == BLOCKS - 1 or (last_piece and q == BLOCKS - 2) for q in range(BLOCKS)]
             widths = [PIECE // 2 if last_piece and q == BLOCKS - 1 else PIECE for q in range(BLOCKS)]
 
             def first(q):

import concourse.mybir as mybir

BF16, F32, U16 = mybir.dt.bfloat16, mybir.dt.float32, mybir.dt.uint16
ACT = mybir.ActivationFunctionType
ALU = mybir.AluOpType

P = 128
LEVELS = 2048
N = 2048
PIECE = 512
N_PIECES = N // PIECE
HIDDEN = 512
BLOCKS = HIDDEN // P

FLOPS = 2 * N * (P * 2 * P + P * HIDDEN + HIDDEN * HIDDEN)


def tile_wavenetmodel_kernel(tc, table, w, b_gate, w_skip, b_skip, w_p1, b_p1, offs, out):
    nc = tc.nc
    with (
        tc.tile_pool(name="held", bufs=1) as held,
        tc.tile_pool(name="gated", bufs=N_PIECES) as gated,
        tc.tile_pool(name="hidden", bufs=N_PIECES) as hidden,
        tc.tile_pool(name="work", bufs=12) as work,
        tc.tile_pool(name="outputs", bufs=16) as outputs,
        tc.psum_pool(name="banks", bufs=8) as banks,
    ):
        offsets = held.tile([P, N // 16], U16, name="offsets")
        table_sb = held.tile([P, LEVELS], BF16, name="table_sb")
        w_sb = held.tile([P, 2 * P], BF16, name="w_sb")
        b_gate_sb = held.tile([P, 2], F32, name="b_gate_sb")
        w_skip_sb = held.tile([P, HIDDEN], BF16, name="w_skip_sb")
        b_skip_sb = held.tile([P, BLOCKS], F32, name="b_skip_sb")
        w_p1_sb = held.tile([P, BLOCKS, HIDDEN], BF16, name="w_p1_sb")
        b_p1_sb = held.tile([P, BLOCKS], F32, name="b_p1_sb")
        nc.sync.dma_start(offsets[:], offs)
        nc.sync.dma_start(table_sb[:], table)
        nc.scalar.dma_start(w_sb[:], w)
        with nc.allow_non_contiguous_dma(reason="a bias vector goes one element to a partition"):
            nc.scalar.dma_start(b_gate_sb[:], b_gate.rearrange("(k p) one -> p (k one)", p=P))
            nc.gpsimd.dma_start(b_skip_sb[:], b_skip.rearrange("(k p) one -> p (k one)", p=P))
            nc.gpsimd.dma_start(b_p1_sb[:], b_p1.rearrange("(k p) one -> p (k one)", p=P))
        nc.sync.dma_start(w_skip_sb[:], w_skip)
        nc.sync.dma_start(w_p1_sb[:], w_p1.rearrange("(k p) q -> p k q", p=P))

        zeros = held.tile([P, 1], F32, name="zeros")
        nc.vector.memset(zeros[:], 0.0)
        unread = held.tile([P, 1], F32, name="unread")
        nc.scalar.activation(unread[:], zeros[:], ACT.Tanh)

        w_skip_half = held.tile([P, HIDDEN], BF16, name="w_skip_half")
        nc.vector.tensor_scalar_mul(w_skip_half[:], w_skip_sb[:], 0.5)
        b_sigmoid_half = held.tile([P, 1], F32, name="b_sigmoid_half")
        nc.vector.tensor_scalar_mul(b_sigmoid_half[:], b_gate_sb[:, 0:1], 0.5)

        def elu_first(acc, bias, spare_vector, width=PIECE):
            grown = work.tile([P, width], F32, name="grown")
            nc.scalar.activation(grown[:], acc, ACT.Exp, bias=bias)
            other = work.tile([P, width], F32, name="other")
            if spare_vector:
                nc.scalar.activation(other[:], acc, ACT.Relu, bias=bias)
            else:
                nc.vector.tensor_scalar(other[:], grown[:], 1.0, -1.0, op0=ALU.min, op1=ALU.add)
            return grown, other

        def elu_last(result, acc, bias, grown, other, spare_vector):
            if spare_vector:
                nc.vector.scalar_tensor_tensor(result, grown[:], -1.0, other[:], op0=ALU.add, op1=ALU.min)
            else:
                nc.vector.scalar_tensor_tensor(result, acc, bias, other[:], op0=ALU.add, op1=ALU.max)

        def staggered(first, last):
            for k in range(BLOCKS + 1):
                if k < BLOCKS:
                    first(k)
                if k > 0:
                    last(k - 1)

        def gate(c):
            piece_offsets = offsets[:, c * (PIECE // 16) : (c + 1) * (PIECE // 16)]
            z_sigmoid = banks.tile([P, PIECE], F32, name="z_sigmoid", tag="bank")
            nc.tensor.matmul(z_sigmoid[:], w_sb[:, 0:P], table_sb[:].indirect(piece_offsets), start=True, stop=True)
            z_tanh = banks.tile([P, PIECE], F32, name="z_tanh", tag="bank")
            nc.tensor.matmul(z_tanh[:], w_sb[:, P : 2 * P], table_sb[:].indirect(piece_offsets), start=True, stop=True)
            opening = work.tile([P, PIECE], F32, name="opening")
            nc.scalar.activation(opening[:], z_sigmoid[:], ACT.Tanh, bias=b_sigmoid_half[:], scale=0.5)
            signal = work.tile([P, PIECE], F32, name="signal")
            nc.scalar.activation(signal[:], z_tanh[:], ACT.Tanh, bias=b_gate_sb[:, 1:2])
            u_twice = gated.tile([P, PIECE], BF16, name="u_twice")
            nc.vector.scalar_tensor_tensor(u_twice[:], opening[:], 1.0, signal[:], op0=ALU.add, op1=ALU.mult)
            return u_twice

        def skip(u_twice, strips):
            width = PIECE // strips
            s, terms, h = {}, {}, {}

            def first(k):
                s[k] = banks.tile([P, PIECE], F32, name="s", tag="bank")
                for j in range(0, PIECE, width):
                    nc.tensor.matmul(
                        s[k][:, j : j + width],
                        w_skip_half[:, k * P : (k + 1) * P],
                        u_twice[:, j : j + width],
                        start=True,
                        stop=True,
                    )
                terms[k] = elu_first(s[k][:], b_skip_sb[:, k : k + 1], k == BLOCKS - 1)

            def last(k):
                h[k] = hidden.tile([P, PIECE], BF16, name=f"h{k}")
                elu_last(h[k][:], s[k][:], b_skip_sb[:, k : k + 1], terms[k][0], terms[k][1], k == BLOCKS - 1)

            staggered(first, last)
            return h

        def post(c, h):
            parts = {}
            last_piece = c == N_PIECES - 1
            spares = [q == BLOCKS - 1 or (last_piece and q == BLOCKS - 2) for q in range(BLOCKS)]
            widths = [PIECE // 2 if last_piece and q == BLOCKS - 1 else PIECE for q in range(BLOCKS)]

            def first(q):
                parts[q] = []
                for j in range(0, PIECE, widths[q]):
                    acc = banks.tile([P, widths[q]], F32, name="acc", tag="bank")
                    for k in range(BLOCKS):
                        nc.tensor.matmul(
                            acc[:],
                            w_p1_sb[:, k, q * P : (q + 1) * P],
                            h[k][:, j : j + widths[q]],
                            start=(k == 0),
                            stop=(k == BLOCKS - 1),
                        )
                    grown, other = elu_first(acc[:], b_p1_sb[:, q : q + 1], spares[q], widths[q])
                    parts[q].append((c * PIECE + j, acc, grown, other))

            def last(q):
                for column, acc, grown, other in parts[q]:
                    o = outputs.tile([P, widths[q]], F32, name="o")
                    elu_last(o[:], acc[:], b_p1_sb[:, q : q + 1], grown, other, spares[q])
                    nc.sync.dma_start(out[q * P : (q + 1) * P, column : column + widths[q]], o[:])

            staggered(first, last)

        u_twice, h = {}, {}
        for c in (0, 1):
            u_twice[c] = gate(c)
        for c in (0, 1):
            h[c] = skip(u_twice[c], strips=4)
        u_twice[2] = gate(2)
        post(0, h[0])
        h[2] = skip(u_twice[2], strips=2)
        u_twice[3] = gate(3)
        post(1, h[1])
        h[3] = skip(u_twice[3], strips=1)
        post(2, h[2])
        post(3, h[3])
